import numpy as np
import ml_dtypes


def mxq(x, axis, fmt="e4m3"):
    dtype, down = {"e4m3": (ml_dtypes.float8_e4m3fn, 7), "e5m2": (ml_dtypes.float8_e5m2, 14)}[fmt]
    v = np.moveaxis(np.asarray(x, np.float32).astype(ml_dtypes.bfloat16).astype(np.float64), axis, -1)
    blocks = v.reshape(v.shape[:-1] + (-1, 32))
    amax = np.abs(blocks).max(-1, keepdims=True)
    byte = np.maximum(np.where(amax > 0, np.frexp(amax)[1] - 1 + 127, 0) - down, 1)
    scale = np.exp2(byte - 127.0)
    codes = (blocks / scale).astype(np.float32).astype(dtype).astype(np.float64)
    return np.moveaxis((codes * scale).reshape(v.shape), -1, axis)


WIDE = False


def mx_kscale(k):
    if not WIDE:
        return np.ones(k)
    levels = np.array([10, -10, 5, -5, 0])
    a = np.random.permutation(np.resize(levels, k // 512 * 4)).reshape(k // 512, 4)
    idx = np.arange(k)
    return np.exp2(a[idx // 512, idx % 128 // 32])


BF16 = ml_dtypes.bfloat16


def bf(x):
    return np.asarray(x, np.float32).astype(BF16)


def f64(x):
    return np.asarray(x).astype(np.float64)


B, S, H, QD, KD, R = 4, 2048, 512, 128, 128, 128
SCALING = 2.0


def setup_inputs():
    s = mx_kscale(H)

    def w(o):
        return bf(np.random.standard_normal((o, H)) / np.sqrt(H) / s[None, :])

    def xa():
        return bf(np.random.standard_normal((B, S, R)) * 0.6)

    def up(o):
        return bf(np.random.standard_normal((R, o)) * 0.4 / np.sqrt(R))

    def bias(o):
        return bf(np.random.standard_normal(o) * 0.3)

    return {"x": bf(np.random.standard_normal((B, S, H)) * s),
            "Wq": w(QD), "Wk": w(KD), "Wv": w(KD),
            "bq": bias(QD), "bk": bias(KD), "bv": bias(KD),
            "xa_q": xa(), "xa_k": xa(), "xa_v": xa(),
            "Bq": up(QD), "Bk": up(KD), "Bv": up(KD)}


def lora_proj(xq, W, b, xa, Bm):
    base = xq @ mxq(f64(W), 1, "e4m3").T
    delta = f64(xa) @ f64(Bm)
    return base + SCALING * delta + f64(b)


def reference(x, Wq, Wk, Wv, bq, bk, bv, xa_q, xa_k, xa_v, Bq, Bk, Bv):
    xq = mxq(f64(x), 2, "e4m3")
    q = lora_proj(xq, Wq, bq, xa_q, Bq)
    k = lora_proj(xq, Wk, bk, xa_k, Bk)
    v = lora_proj(xq, Wv, bv, xa_v, Bv)
    return q, k, v

@@ -1,0 +1,278 @@
+from contextlib import ExitStack
+
+import concourse.mybir as mybir
+from concourse.masks import make_identity
+
+F32 = mybir.dt.float32
+BF16 = mybir.dt.bfloat16
+U32 = mybir.dt.uint32
+U8 = mybir.dt.uint8
+FP8X4 = mybir.dt.float8_e4m3fn_x4
+ADD = mybir.AluOpType.add
+MULT = mybir.AluOpType.mult
+
+P = 128
+TOKENS = 8192
+HID = 512
+OUT = 128
+RANK = 128
+KINDS = 3
+NT = TOKENS // P
+QUAD = 4
+NQ = NT // QUAD
+BANKS = 8
+SCALING = 2.0
+
+FLOPS = 2 * TOKENS * KINDS * OUT * (HID + RANK)
+
+X_CHUNKS = [4, 4, 8, 8, 8, 8, 8, 8, 8]
+XA_CHUNKS = [4, 4, 8, 16, 16, 16]
+LOAD_ORDER = [
+    ("xa", 0), ("w", 0), ("x", 0), ("xa", 1), ("x", 1), ("xa", 2), ("x", 2), ("xa", 3), ("x", 3),
+    ("x", 4), ("xa", 4), ("x", 5), ("x", 6), ("xa", 5), ("x", 7), ("x", 8),
+]
+RES_TILES = 8
+
+
+def tile_loraqkvlinear_pa_t_kernel(
+    tc, x, Wq, Wk, Wv, bq, bk, bv, xa_q, xa_k, xa_v, Bq, Bk, Bv, out_0, out_1, out_2
+):
+    nc = tc.nc
+    xv = x.flatten_outer_dims().rearrange("(p j) h -> p j h", j=NT)
+    xav = [a.flatten_outer_dims().rearrange("(p j) r -> p j r", j=NT) for a in (xa_q, xa_k, xa_v)]
+    ov = [o.flatten_outer_dims().rearrange("(p j) o -> p j o", j=NT) for o in (out_0, out_1, out_2)]
+    ws = (Wq, Wk, Wv)
+    bs = (bq, bk, bv)
+    ups = (Bq, Bk, Bv)
+
+    with ExitStack() as ctx:
+        consts = ctx.enter_context(tc.tile_pool(name="consts", bufs=1))
+        inputs = ctx.enter_context(tc.tile_pool(name="inputs", bufs=1))
+        ring2 = ctx.enter_context(tc.tile_pool(name="ring2", bufs=2))
+        ring3 = ctx.enter_context(tc.tile_pool(name="ring3", bufs=3))
+        results = ctx.enter_context(tc.tile_pool(name="results", bufs=5))
+        psum = ctx.enter_context(tc.psum_pool(name="psum", bufs=1))
+        ctx.enter_context(tc.manual_schedule())
+
+        ident_f = consts.tile([P, P], F32, name="ident_f")
+        make_identity(nc, ident_f[:])
+        ident_b = consts.tile([P, P], BF16, name="ident_b")
+        make_identity(nc, ident_b[:])
+
+        up_sb = consts.tile([P, KINDS, OUT], BF16, name="up_sb")
+        bias_bf = consts.tile([P, KINDS, OUT], BF16, name="bias_bf")
+        for k in range(KINDS):
+            nc.scalar.dma_start(out=up_sb[:, k, :], in_=ups[k])
+        for k in range(KINDS):
+            nc.scalar.dma_start(out=bias_bf[:, k, :], in_=bs[k].partition_broadcast(P))
+
+        warm = consts.tile([P, 2], F32, name="warm")
+        nc.vector.memset(warm[:, 0:1], 0.0)
+        nc.scalar.mul(out=warm[:, 1:2], in_=warm[:, 0:1], mul=SCALING)
+
+        w_sb = inputs.tile([P, KINDS, HID], BF16, name="w_sb")
+        x_of = {}
+        xa_of = {}
+        x_tiles = []
+        j0 = 0
+        for c, n in enumerate(X_CHUNKS):
+            xc = inputs.tile([P, n, HID], BF16, name="x%d" % c)
+            x_tiles.append((xc, j0, n))
+            for i in range(n):
+                x_of[j0 + i] = (xc, i)
+            j0 += n
+        xa_tiles = []
+        j0 = 0
+        for c, n in enumerate(XA_CHUNKS):
+            group = []
+            for k in range(KINDS):
+                xac = inputs.tile([P, n, RANK], BF16, name="xa%d_%d" % (k, c))
+                group.append(xac)
+                for i in range(n):
+                    xa_of[(k, j0 + i)] = (xac, i)
+            xa_tiles.append((group, j0, n))
+            j0 += n
+        for what, c in LOAD_ORDER:
+            if what == "w":
+                for k in range(KINDS):
+                    nc.sync.dma_start(out=w_sb[:, k, :], in_=ws[k])
+            elif what == "x":
+                xc, j0, n = x_tiles[c]
+                nc.sync.dma_start(out=xc[:], in_=xv[:, j0 : j0 + n, :])
+            else:
+                group, j0, n = xa_tiles[c]
+                for k in range(KINDS):
+                    nc.sync.dma_start(out=group[k][:], in_=xav[k][:, j0 : j0 + n, :])
+
+        count = [0]
+
+        def bank(shape, dtype):
+            i = count[0] % BANKS
+            count[0] += 1
+            return psum.tile(shape, dtype, name="bank%d" % i, tag="bank%d" % i)
+
+        codes = {}
+        planes = {}
+        xaT = {}
+        tt = {}
+        mb = {}
+        res = {}
+
+        def valid(g):
+            return 0 <= g < NQ
+
+        def word_transposes(srcs):
+            xt = bank([P, 2, 2, P], F32)
+            for i, src in enumerate(srcs):
+                words = src.bitcast(F32)
+                for u in range(2):
+                    nc.tensor.transpose(xt[:, i, u, :], words[:, u * P : (u + 1) * P], ident_f[:])
+            return xt
+
+        def copy_words(grouped, first, n, xt):
+            view = grouped[:].bitcast(F32).rearrange("p (t r u) -> p t r u", r=P, u=2)
+            nc.scalar.copy(
+                out=view[:, first : first + n, :, :],
+                in_=xt[:, 0:n, :, :].rearrange("p t u r -> p t r u"),
+            )
+
+        w_grouped = consts.tile([P, KINDS * HID], BF16, name="w_grouped", align_bytes=64)
+        w_codes = consts.tile([P, KINDS * OUT], U32, name="w_codes", align_bytes=64)
+        w_planes = consts.tile([P, KINDS * OUT], U8, name="w_planes", align_bytes=64)
+        bias_f = consts.tile([P, KINDS, QUAD, OUT], F32, name="bias_f")
+
+        def weights_pe():
+            return [word_transposes([w_sb[:, 0, :], w_sb[:, 1, :]]), word_transposes([w_sb[:, 2, :]])]
+
+        def weights_rest(wt):
+            copy_words(w_grouped, 0, 2, wt[0])
+            copy_words(w_grouped, 2, 1, wt[1])
+            nc.vector.quantize_mx(
+                out=w_codes[:, 0 : 2 * OUT].bitcast(FP8X4),
+                scales=w_planes[:, 0 : 2 * OUT],
+                in_=w_grouped[:, 0 : 2 * HID],
+            )
+            nc.vector.quantize_mx(
+                out=w_codes[:, 2 * OUT : 3 * OUT].bitcast(FP8X4),
+                scales=w_planes[:, 2 * OUT : 3 * OUT],
+                in_=w_grouped[:, 2 * HID : 3 * HID],
+            )
+            nc.vector.tensor_copy(
+                out=bias_f[:], in_=bias_bf[:].unsqueeze(2).to_broadcast([P, KINDS, QUAD, OUT])
+            )
+
+        def x_src(j):
+            xc, i = x_of[j]
+            return xc[:, i, :]
+
+        def tx_pe(g):
+            return [word_transposes([x_src(QUAD * g + 2 * h), x_src(QUAD * g + 2 * h + 1)]) for h in range(2)]
+
+        def txa_pe(g):
+            out = []
+            for h in range(2):
+                xat = bank([P, 6, P], BF16)
+                for s in range(6):
+                    k, i = divmod(6 * h + s, QUAD)
+                    xac, loc = xa_of[(k, QUAD * g + i)]
+                    nc.tensor.transpose(xat[:, s, :], xac[:, loc, :], ident_b[:])
+                out.append(xat)
+            return out
+
+        def delta_pe(g):
+            out = []
+            for k in range(KINDS):
+                d = bank([P, QUAD, OUT], F32)
+                for i in range(QUAD):
+                    nc.tensor.matmul(
+                        d[:, i, :], lhsT=xaT[g][:, QUAD * k + i, :], rhs=up_sb[:, k, :], start=True, stop=True
+                    )
+                out.append(d)
+            return out
+
+        def base_pe(g):
+            for k in range(KINDS):
+                m = bank([P, QUAD, OUT], F32)
+                for i in range(QUAD):
+                    nc.tensor.matmul_mx(
+                        out=m[:, i, :],
+                        lhsT=codes[g][:, i * P : (i + 1) * P].bitcast(FP8X4),
+                        lhsT_scale=planes[g][:, i * P : (i + 1) * P],
+                        rhs=w_codes[:, k * OUT : (k + 1) * OUT].bitcast(FP8X4),
+                        rhs_scale=w_planes[:, k * OUT : (k + 1) * OUT],
+                        start=True,
+                        stop=True,
+                    )
+                mb[(g, k)] = m
+
+        def delta_out_vector(g, k, d):
+            t = ring3.tile([P, QUAD, OUT], F32, name="t%d" % k)
+            nc.vector.scalar_tensor_tensor(
+                out=t[:].rearrange("p a b -> p (a b)"),
+                in0=d[:].rearrange("p a b -> p (a b)"),
+                scalar=SCALING,
+                in1=bias_f[:, k, :, :].rearrange("p a b -> p (a b)"),
+                op0=MULT,
+                op1=ADD,
+            )
+            tt[(g, k)] = t
+
+        def delta_out_scalar(g, k, d):
+            t = ring3.tile([P, QUAD, OUT], F32, name="t%d" % k)
+            nc.scalar.mul(out=t[:], in_=d[:], mul=SCALING)
+            tt[(g, k)] = t
+
+        def bias_gpsimd(g, k):
+            t = tt[(g, k)]
+            nc.gpsimd.tensor_tensor(out=t[:], in0=t[:], in1=bias_f[:, k, :, :], op=ADD)
+
+        def base_out(g, k):
+            c, half = divmod(g, RES_TILES // QUAD)
+            if (c, k) not in res:
+                res[(c, k)] = results.tile([P, RES_TILES, OUT], F32, name="res%d" % k)
+            r = res[(c, k)]
+            nc.vector.tensor_tensor(
+                out=r[:, half * QUAD : (half + 1) * QUAD, :], in0=mb[(g, k)][:], in1=tt[(g, k)][:], op=ADD
+            )
+            if half == RES_TILES // QUAD - 1:
+                nc.sync.dma_start(out=ov[k][:, c * RES_TILES : (c + 1) * RES_TILES, :], in_=r[:])
+
+        for g in range(-2, NQ + 1):
+            if valid(g + 1):
+                xts = tx_pe(g + 1)
+            if valid(g - 1):
+                base_out(g - 1, 1)
+                base_out(g - 1, 2)
+            if valid(g + 1):
+                grouped = ring2.tile([P, QUAD * HID], BF16, name="grouped", align_bytes=64)
+                copy_words(grouped, 0, 2, xts[0])
+                copy_words(grouped, 2, 2, xts[1])
+                ds = delta_pe(g + 1)
+                delta_out_vector(g + 1, 0, ds[0])
+                delta_out_scalar(g + 1, 1, ds[1])
+                cw = ring2.tile([P, QUAD * P], U32, name="cw", align_bytes=64)
+                pl = ring2.tile([P, QUAD * P], U8, name="pl", align_bytes=64)
+                nc.vector.quantize_mx(out=cw[:].bitcast(FP8X4), scales=pl[:], in_=grouped[:])
+                codes[g + 1] = cw
+                planes[g + 1] = pl
+            if valid(g + 2):
+                xats = txa_pe(g + 2)
+            if g == -2:
+                wt = weights_pe()
+            if valid(g + 1):
+                bias_gpsimd(g + 1, 1)
+            if valid(g + 2):
+                xa_t = ring2.tile([P, KINDS * QUAD, P], BF16, name="xa_t")
+                nc.scalar.copy(out=xa_t[:, 0:6, :], in_=xats[0][:])
+                nc.scalar.copy(out=xa_t[:, 6:12, :], in_=xats[1][:])
+                xaT[g + 2] = xa_t
+            if g == -2:
+                weights_rest(wt)
+            if valid(g + 1):
+                delta_out_scalar(g + 1, 2, ds[2])
+            if valid(g):
+                base_pe(g)
+            if valid(g + 1):
+                bias_gpsimd(g + 1, 2)
+            if valid(g):
+                base_out(g, 0)

@@ -32,6 +32,7 @@ LOAD_ORDER = [
     ("x", 4), ("xa", 4), ("x", 5), ("x", 6), ("xa", 5), ("x", 7), ("x", 8),
 ]
 RES_TILES = 8
+TAPER = 2
 
 
 def tile_loraqkvlinear_pa_t_kernel(
@@ -234,12 +235,19 @@ def tile_loraqkvlinear_pa_t_kernel(
             nc.vector.tensor_tensor(
                 out=r[:, half * QUAD : (half + 1) * QUAD, :], in0=mb[(g, k)][:], in1=tt[(g, k)][:], op=ADD
             )
-            if half == RES_TILES // QUAD - 1:
+            if g >= NQ - TAPER:
+                j0 = g * QUAD
+                nc.sync.dma_start(out=ov[k][:, j0 : j0 + QUAD, :], in_=r[:, half * QUAD : (half + 1) * QUAD, :])
+            elif half == RES_TILES // QUAD - 1:
                 nc.sync.dma_start(out=ov[k][:, c * RES_TILES : (c + 1) * RES_TILES, :], in_=r[:])
 
         for g in range(-2, NQ + 1):
             if valid(g + 1):
                 xts = tx_pe(g + 1)
+            if valid(g + 2):
+                xats = txa_pe(g + 2)
+            if g == -2:
+                wt = weights_pe()
             if valid(g - 1):
                 base_out(g - 1, 1)
                 base_out(g - 1, 2)
@@ -247,20 +255,6 @@ def tile_loraqkvlinear_pa_t_kernel(
                 grouped = ring2.tile([P, QUAD * HID], BF16, name="grouped", align_bytes=64)
                 copy_words(grouped, 0, 2, xts[0])
                 copy_words(grouped, 2, 2, xts[1])
-                ds = delta_pe(g + 1)
-                delta_out_vector(g + 1, 0, ds[0])
-                delta_out_scalar(g + 1, 1, ds[1])
-                cw = ring2.tile([P, QUAD * P], U32, name="cw", align_bytes=64)
-                pl = ring2.tile([P, QUAD * P], U8, name="pl", align_bytes=64)
-                nc.vector.quantize_mx(out=cw[:].bitcast(FP8X4), scales=pl[:], in_=grouped[:])
-                codes[g + 1] = cw
-                planes[g + 1] = pl
-            if valid(g + 2):
-                xats = txa_pe(g + 2)
-            if g == -2:
-                wt = weights_pe()
-            if valid(g + 1):
-                bias_gpsimd(g + 1, 1)
             if valid(g + 2):
                 xa_t = ring2.tile([P, KINDS * QUAD, P], BF16, name="xa_t")
                 nc.scalar.copy(out=xa_t[:, 0:6, :], in_=xats[0][:])
@@ -269,6 +263,15 @@ def tile_loraqkvlinear_pa_t_kernel(
             if g == -2:
                 weights_rest(wt)
             if valid(g + 1):
+                ds = delta_pe(g + 1)
+                delta_out_vector(g + 1, 0, ds[0])
+                delta_out_scalar(g + 1, 1, ds[1])
+                cw = ring2.tile([P, QUAD * P], U32, name="cw", align_bytes=64)
+                pl = ring2.tile([P, QUAD * P], U8, name="pl", align_bytes=64)
+                nc.vector.quantize_mx(out=cw[:].bitcast(FP8X4), scales=pl[:], in_=grouped[:])
+                codes[g + 1] = cw
+                planes[g + 1] = pl
+                bias_gpsimd(g + 1, 1)
                 delta_out_scalar(g + 1, 2, ds[2])
             if valid(g):
                 base_pe(g)

@@ -25,14 +25,13 @@ SCALING = 2.0
 
 FLOPS = 2 * TOKENS * KINDS * OUT * (HID + RANK)
 
-X_CHUNKS = [4, 4, 8, 8, 8, 8, 8, 8, 8]
-XA_CHUNKS = [4, 4, 8, 16, 16, 16]
+X_CHUNKS = [4, 4, 8, 16, 16, 16]
+XA_CHUNKS = [8, 8, 16, 32]
 LOAD_ORDER = [
-    ("xa", 0), ("w", 0), ("x", 0), ("xa", 1), ("x", 1), ("xa", 2), ("x", 2), ("xa", 3), ("x", 3),
-    ("x", 4), ("xa", 4), ("x", 5), ("x", 6), ("xa", 5), ("x", 7), ("x", 8),
+    ("x", 0), ("xa", 0), ("w", 0), ("x", 1), ("xa", 1), ("x", 2), ("xa", 2), ("x", 3), ("xa", 3), ("x", 4), ("x", 5),
 ]
-RES_TILES = 8
-TAPER = 2
+RES_QUADS = 4
+STORE_AFTER = {3: 4, 7: 4, 11: 4, 13: 2, 14: 1, 15: 1}
 
 
 def tile_loraqkvlinear_pa_t_kernel(
@@ -50,8 +49,7 @@ def tile_loraqkvlinear_pa_t_kernel(
         consts = ctx.enter_context(tc.tile_pool(name="consts", bufs=1))
         inputs = ctx.enter_context(tc.tile_pool(name="inputs", bufs=1))
         ring2 = ctx.enter_context(tc.tile_pool(name="ring2", bufs=2))
-        ring3 = ctx.enter_context(tc.tile_pool(name="ring3", bufs=3))
-        results = ctx.enter_context(tc.tile_pool(name="results", bufs=5))
+        results = ctx.enter_context(tc.tile_pool(name="results", bufs=3))
         psum = ctx.enter_context(tc.psum_pool(name="psum", bufs=1))
         ctx.enter_context(tc.manual_schedule())
 
@@ -63,9 +61,9 @@ def tile_loraqkvlinear_pa_t_kernel(
         up_sb = consts.tile([P, KINDS, OUT], BF16, name="up_sb")
         bias_bf = consts.tile([P, KINDS, OUT], BF16, name="bias_bf")
         for k in range(KINDS):
-            nc.scalar.dma_start(out=up_sb[:, k, :], in_=ups[k])
+            nc.gpsimd.dma_start(out=up_sb[:, k, :], in_=ups[k])
         for k in range(KINDS):
-            nc.scalar.dma_start(out=bias_bf[:, k, :], in_=bs[k].partition_broadcast(P))
+            nc.gpsimd.dma_start(out=bias_bf[:, k, :], in_=bs[k].partition_broadcast(P))
 
         warm = consts.tile([P, 2], F32, name="warm")
         nc.vector.memset(warm[:, 0:1], 0.0)
@@ -158,9 +156,6 @@ def tile_loraqkvlinear_pa_t_kernel(
                 scales=w_planes[:, 2 * OUT : 3 * OUT],
                 in_=w_grouped[:, 2 * HID : 3 * HID],
             )
-            nc.vector.tensor_copy(
-                out=bias_f[:], in_=bias_bf[:].unsqueeze(2).to_broadcast([P, KINDS, QUAD, OUT])
-            )
 
         def x_src(j):
             xc, i = x_of[j]
@@ -207,7 +202,7 @@ def tile_loraqkvlinear_pa_t_kernel(
                 mb[(g, k)] = m
 
         def delta_out_vector(g, k, d):
-            t = ring3.tile([P, QUAD, OUT], F32, name="t%d" % k)
+            t = ring2.tile([P, QUAD, OUT], F32, name="t%d" % k)
             nc.vector.scalar_tensor_tensor(
                 out=t[:].rearrange("p a b -> p (a b)"),
                 in0=d[:].rearrange("p a b -> p (a b)"),
@@ -219,7 +214,7 @@ def tile_loraqkvlinear_pa_t_kernel(
             tt[(g, k)] = t
 
         def delta_out_scalar(g, k, d):
-            t = ring3.tile([P, QUAD, OUT], F32, name="t%d" % k)
+            t = ring2.tile([P, QUAD, OUT], F32, name="t%d" % k)
             nc.scalar.mul(out=t[:], in_=d[:], mul=SCALING)
             tt[(g, k)] = t
 
@@ -228,22 +223,23 @@ def tile_loraqkvlinear_pa_t_kernel(
             nc.gpsimd.tensor_tensor(out=t[:], in0=t[:], in1=bias_f[:, k, :, :], op=ADD)
 
         def base_out(g, k):
-            c, half = divmod(g, RES_TILES // QUAD)
+            c, part = divmod(g, RES_QUADS)
             if (c, k) not in res:
-                res[(c, k)] = results.tile([P, RES_TILES, OUT], F32, name="res%d" % k)
+                res[(c, k)] = results.tile([P, RES_QUADS * QUAD, OUT], F32, name="res%d" % k)
             r = res[(c, k)]
             nc.vector.tensor_tensor(
-                out=r[:, half * QUAD : (half + 1) * QUAD, :], in0=mb[(g, k)][:], in1=tt[(g, k)][:], op=ADD
+                out=r[:, part * QUAD : (part + 1) * QUAD, :], in0=mb[(g, k)][:], in1=tt[(g, k)][:], op=ADD
             )
-            if g >= NQ - TAPER:
-                j0 = g * QUAD
-                nc.sync.dma_start(out=ov[k][:, j0 : j0 + QUAD, :], in_=r[:, half * QUAD : (half + 1) * QUAD, :])
-            elif half == RES_TILES // QUAD - 1:
-                nc.sync.dma_start(out=ov[k][:, c * RES_TILES : (c + 1) * RES_TILES, :], in_=r[:])
+            if g in STORE_AFTER:
+                n = STORE_AFTER[g] * QUAD
+                j1 = (g + 1) * QUAD
+                l1 = (part + 1) * QUAD
+                nc.sync.dma_start(out=ov[k][:, j1 - n : j1, :], in_=r[:, l1 - n : l1, :])
 
         for g in range(-2, NQ + 1):
-            if valid(g + 1):
-                xts = tx_pe(g + 1)
+            tq = 0 if g == -2 else (g + 1 if g >= 0 else -1)
+            if valid(tq):
+                xts = tx_pe(tq)
             if valid(g + 2):
                 xats = txa_pe(g + 2)
             if g == -2:
@@ -251,7 +247,7 @@ def tile_loraqkvlinear_pa_t_kernel(
             if valid(g - 1):
                 base_out(g - 1, 1)
                 base_out(g - 1, 2)
-            if valid(g + 1):
+            if valid(tq):
                 grouped = ring2.tile([P, QUAD * HID], BF16, name="grouped", align_bytes=64)
                 copy_words(grouped, 0, 2, xts[0])
                 copy_words(grouped, 2, 2, xts[1])
@@ -260,17 +256,23 @@ def tile_loraqkvlinear_pa_t_kernel(
                 nc.scalar.copy(out=xa_t[:, 0:6, :], in_=xats[0][:])
                 nc.scalar.copy(out=xa_t[:, 6:12, :], in_=xats[1][:])
                 xaT[g + 2] = xa_t
-            if g == -2:
-                weights_rest(wt)
             if valid(g + 1):
                 ds = delta_pe(g + 1)
+                if g == -1:
+                    nc.vector.tensor_copy(
+                        out=bias_f[:], in_=bias_bf[:].unsqueeze(2).to_broadcast([P, KINDS, QUAD, OUT])
+                    )
                 delta_out_vector(g + 1, 0, ds[0])
                 delta_out_scalar(g + 1, 1, ds[1])
+            if valid(tq):
                 cw = ring2.tile([P, QUAD * P], U32, name="cw", align_bytes=64)
                 pl = ring2.tile([P, QUAD * P], U8, name="pl", align_bytes=64)
                 nc.vector.quantize_mx(out=cw[:].bitcast(FP8X4), scales=pl[:], in_=grouped[:])
-                codes[g + 1] = cw
-                planes[g + 1] = pl
+                codes[tq] = cw
+                planes[tq] = pl
+            if g == -2:
+                weights_rest(wt)
+            if valid(g + 1):
                 bias_gpsimd(g + 1, 1)
                 delta_out_scalar(g + 1, 2, ds[2])
             if valid(g):

@@ -61,9 +61,9 @@ def tile_loraqkvlinear_pa_t_kernel(
         up_sb = consts.tile([P, KINDS, OUT], BF16, name="up_sb")
         bias_bf = consts.tile([P, KINDS, OUT], BF16, name="bias_bf")
         for k in range(KINDS):
-            nc.gpsimd.dma_start(out=up_sb[:, k, :], in_=ups[k])
+            nc.scalar.dma_start(out=up_sb[:, k, :], in_=ups[k])
         for k in range(KINDS):
-            nc.gpsimd.dma_start(out=bias_bf[:, k, :], in_=bs[k].partition_broadcast(P))
+            nc.scalar.dma_start(out=bias_bf[:, k, :], in_=bs[k].partition_broadcast(P))
 
         warm = consts.tile([P, 2], F32, name="warm")
         nc.vector.memset(warm[:, 0:1], 0.0)

@@ -25,13 +25,14 @@ SCALING = 2.0
 
 FLOPS = 2 * TOKENS * KINDS * OUT * (HID + RANK)
 
-X_CHUNKS = [4, 4, 8, 16, 16, 16]
-XA_CHUNKS = [8, 8, 16, 32]
+X_CHUNKS = [4, 4, 8, 8, 8, 8, 8, 8, 8]
+XA_CHUNKS = [4, 4, 8, 16, 16, 16]
 LOAD_ORDER = [
-    ("x", 0), ("xa", 0), ("w", 0), ("x", 1), ("xa", 1), ("x", 2), ("xa", 2), ("x", 3), ("xa", 3), ("x", 4), ("x", 5),
+    ("xa", 0), ("w", 0), ("x", 0), ("xa", 1), ("x", 1), ("xa", 2), ("x", 2), ("xa", 3), ("x", 3),
+    ("x", 4), ("xa", 4), ("x", 5), ("x", 6), ("xa", 5), ("x", 7), ("x", 8),
 ]
-RES_QUADS = 4
-STORE_AFTER = {3: 4, 7: 4, 11: 4, 13: 2, 14: 1, 15: 1}
+RES_TILES = 8
+TAPER = 2
 
 
 def tile_loraqkvlinear_pa_t_kernel(
@@ -49,7 +50,8 @@ def tile_loraqkvlinear_pa_t_kernel(
         consts = ctx.enter_context(tc.tile_pool(name="consts", bufs=1))
         inputs = ctx.enter_context(tc.tile_pool(name="inputs", bufs=1))
         ring2 = ctx.enter_context(tc.tile_pool(name="ring2", bufs=2))
-        results = ctx.enter_context(tc.tile_pool(name="results", bufs=3))
+        ring3 = ctx.enter_context(tc.tile_pool(name="ring3", bufs=3))
+        results = ctx.enter_context(tc.tile_pool(name="results", bufs=5))
         psum = ctx.enter_context(tc.psum_pool(name="psum", bufs=1))
         ctx.enter_context(tc.manual_schedule())
 
@@ -156,6 +158,9 @@ def tile_loraqkvlinear_pa_t_kernel(
                 scales=w_planes[:, 2 * OUT : 3 * OUT],
                 in_=w_grouped[:, 2 * HID : 3 * HID],
             )
+            nc.vector.tensor_copy(
+                out=bias_f[:], in_=bias_bf[:].unsqueeze(2).to_broadcast([P, KINDS, QUAD, OUT])
+            )
 
         def x_src(j):
             xc, i = x_of[j]
@@ -202,7 +207,7 @@ def tile_loraqkvlinear_pa_t_kernel(
                 mb[(g, k)] = m
 
         def delta_out_vector(g, k, d):
-            t = ring2.tile([P, QUAD, OUT], F32, name="t%d" % k)
+            t = ring3.tile([P, QUAD, OUT], F32, name="t%d" % k)
             nc.vector.scalar_tensor_tensor(
                 out=t[:].rearrange("p a b -> p (a b)"),
                 in0=d[:].rearrange("p a b -> p (a b)"),
@@ -214,7 +219,7 @@ def tile_loraqkvlinear_pa_t_kernel(
             tt[(g, k)] = t
 
         def delta_out_scalar(g, k, d):
-            t = ring2.tile([P, QUAD, OUT], F32, name="t%d" % k)
+            t = ring3.tile([P, QUAD, OUT], F32, name="t%d" % k)
             nc.scalar.mul(out=t[:], in_=d[:], mul=SCALING)
             tt[(g, k)] = t
 
@@ -223,23 +228,22 @@ def tile_loraqkvlinear_pa_t_kernel(
             nc.gpsimd.tensor_tensor(out=t[:], in0=t[:], in1=bias_f[:, k, :, :], op=ADD)
 
         def base_out(g, k):
-            c, part = divmod(g, RES_QUADS)
+            c, half = divmod(g, RES_TILES // QUAD)
             if (c, k) not in res:
-                res[(c, k)] = results.tile([P, RES_QUADS * QUAD, OUT], F32, name="res%d" % k)
+                res[(c, k)] = results.tile([P, RES_TILES, OUT], F32, name="res%d" % k)
             r = res[(c, k)]
             nc.vector.tensor_tensor(
-                out=r[:, part * QUAD : (part + 1) * QUAD, :], in0=mb[(g, k)][:], in1=tt[(g, k)][:], op=ADD
+                out=r[:, half * QUAD : (half + 1) * QUAD, :], in0=mb[(g, k)][:], in1=tt[(g, k)][:], op=ADD
             )
-            if g in STORE_AFTER:
-                n = STORE_AFTER[g] * QUAD
-                j1 = (g + 1) * QUAD
-                l1 = (part + 1) * QUAD
-                nc.sync.dma_start(out=ov[k][:, j1 - n : j1, :], in_=r[:, l1 - n : l1, :])
+            if g >= NQ - TAPER:
+                j0 = g * QUAD
+                nc.sync.dma_start(out=ov[k][:, j0 : j0 + QUAD, :], in_=r[:, half * QUAD : (half + 1) * QUAD, :])
+            elif half == RES_TILES // QUAD - 1:
+                nc.sync.dma_start(out=ov[k][:, c * RES_TILES : (c + 1) * RES_TILES, :], in_=r[:])
 
         for g in range(-2, NQ + 1):
-            tq = 0 if g == -2 else (g + 1 if g >= 0 else -1)
-            if valid(tq):
-                xts = tx_pe(tq)
+            if valid(g + 1):
+                xts = tx_pe(g + 1)
             if valid(g + 2):
                 xats = txa_pe(g + 2)
             if g == -2:
@@ -247,32 +251,26 @@ def tile_loraqkvlinear_pa_t_kernel(
             if valid(g - 1):
                 base_out(g - 1, 1)
                 base_out(g - 1, 2)
-            if valid(tq):
+            if valid(g + 1):
                 grouped = ring2.tile([P, QUAD * HID], BF16, name="grouped", align_bytes=64)
                 copy_words(grouped, 0, 2, xts[0])
                 copy_words(grouped, 2, 2, xts[1])
             if valid(g + 2):
                 xa_t = ring2.tile([P, KINDS * QUAD, P], BF16, name="xa_t")
-                nc.scalar.copy(out=xa_t[:, 0:6, :], in_=xats[0][:])
-                nc.scalar.copy(out=xa_t[:, 6:12, :], in_=xats[1][:])
+                nc.scalar.copy(out=xa_t[:, 0:6, :].bitcast(F32), in_=xats[0][:].bitcast(F32))
+                nc.scalar.copy(out=xa_t[:, 6:12, :].bitcast(F32), in_=xats[1][:].bitcast(F32))
                 xaT[g + 2] = xa_t
-            if valid(g + 1):
-                ds = delta_pe(g + 1)
-                if g == -1:
-                    nc.vector.tensor_copy(
-                        out=bias_f[:], in_=bias_bf[:].unsqueeze(2).to_broadcast([P, KINDS, QUAD, OUT])
-                    )
-                delta_out_vector(g + 1, 0, ds[0])
-                delta_out_scalar(g + 1, 1, ds[1])
-            if valid(tq):
-                cw = ring2.tile([P, QUAD * P], U32, name="cw", align_bytes=64)
-                pl = ring2.tile([P, QUAD * P], U8, name="pl", align_bytes=64)
-                nc.vector.quantize_mx(out=cw[:].bitcast(FP8X4), scales=pl[:], in_=grouped[:])
-                codes[tq] = cw
-                planes[tq] = pl
             if g == -2:
                 weights_rest(wt)
             if valid(g + 1):
+                ds = delta_pe(g + 1)
+                delta_out_vector(g + 1, 0, ds[0])
+                delta_out_scalar(g + 1, 1, ds[1])
+                cw = ring2.tile([P, QUAD * P], U32, name="cw", align_bytes=64)
+                pl = ring2.tile([P, QUAD * P], U8, name="pl", align_bytes=64)
+                nc.vector.quantize_mx(out=cw[:].bitcast(FP8X4), scales=pl[:], in_=grouped[:])
+                codes[g + 1] = cw
+                planes[g + 1] = pl
                 bias_gpsimd(g + 1, 1)
                 delta_out_scalar(g + 1, 2, ds[2])
             if valid(g):

@@ -28,8 +28,7 @@ FLOPS = 2 * TOKENS * KINDS * OUT * (HID + RANK)
 X_CHUNKS = [4, 4, 8, 8, 8, 8, 8, 8, 8]
 XA_CHUNKS = [4, 4, 8, 16, 16, 16]
 LOAD_ORDER = [
-    ("xa", 0), ("w", 0), ("x", 0), ("xa", 1), ("x", 1), ("xa", 2), ("x", 2), ("xa", 3), ("x", 3),
-    ("x", 4), ("xa", 4), ("x", 5), ("x", 6), ("xa", 5), ("x", 7), ("x", 8),
+    ("xa", 0), ("w", 0), ("x", 0), ("up", 0), ("bias", 0), ("xa", 1), ("x", 1), ("xa", 2), ("x", 2), ("xa", 3), ("x", 3), ("x", 4), ("xa", 4), ("x", 5), ("x", 6), ("xa", 5), ("x", 7), ("x", 8),
 ]
 RES_TILES = 8
 TAPER = 2
@@ -62,10 +61,6 @@ def tile_loraqkvlinear_pa_t_kernel(
 
         up_sb = consts.tile([P, KINDS, OUT], BF16, name="up_sb")
         bias_bf = consts.tile([P, KINDS, OUT], BF16, name="bias_bf")
-        for k in range(KINDS):
-            nc.scalar.dma_start(out=up_sb[:, k, :], in_=ups[k])
-        for k in range(KINDS):
-            nc.scalar.dma_start(out=bias_bf[:, k, :], in_=bs[k].partition_broadcast(P))
 
         warm = consts.tile([P, 2], F32, name="warm")
         nc.vector.memset(warm[:, 0:1], 0.0)
@@ -97,6 +92,12 @@ def tile_loraqkvlinear_pa_t_kernel(
             if what == "w":
                 for k in range(KINDS):
                     nc.sync.dma_start(out=w_sb[:, k, :], in_=ws[k])
+            elif what == "up":
+                for k in range(KINDS):
+                    nc.sync.dma_start(out=up_sb[:, k, :], in_=ups[k])
+            elif what == "bias":
+                for k in range(KINDS):
+                    nc.sync.dma_start(out=bias_bf[:, k, :], in_=bs[k].partition_broadcast(P))
             elif what == "x":
                 xc, j0, n = x_tiles[c]
                 nc.sync.dma_start(out=xc[:], in_=xv[:, j0 : j0 + n, :])
@@ -158,8 +159,13 @@ def tile_loraqkvlinear_pa_t_kernel(
                 scales=w_planes[:, 2 * OUT : 3 * OUT],
                 in_=w_grouped[:, 2 * HID : 3 * HID],
             )
-            nc.vector.tensor_copy(
-                out=bias_f[:], in_=bias_bf[:].unsqueeze(2).to_broadcast([P, KINDS, QUAD, OUT])
+            nc.gpsimd.tensor_scalar(
+                out=bias_f[:],
+                in0=bias_bf[:].unsqueeze(2).to_broadcast([P, KINDS, QUAD, OUT]),
+                scalar1=1.0,
+                scalar2=0.0,
+                op0=MULT,
+                op1=ADD,
             )
 
         def x_src(j):

@@ -60,7 +60,10 @@ def tile_loraqkvlinear_pa_t_kernel(
         make_identity(nc, ident_b[:])
 
         up_sb = consts.tile([P, KINDS, OUT], BF16, name="up_sb")
-        bias_bf = consts.tile([P, KINDS, OUT], BF16, name="bias_bf")
+        bias_row = consts.tile([P, KINDS, OUT], BF16, name="bias_row")
+        nc.vector.memset(bias_row[:], 0.0)
+        ones = consts.tile([P, P], BF16, name="ones")
+        nc.vector.memset(ones[:], 1.0)
 
         warm = consts.tile([P, 2], F32, name="warm")
         nc.vector.memset(warm[:, 0:1], 0.0)
@@ -97,7 +100,7 @@ def tile_loraqkvlinear_pa_t_kernel(
                     nc.sync.dma_start(out=up_sb[:, k, :], in_=ups[k])
             elif what == "bias":
                 for k in range(KINDS):
-                    nc.sync.dma_start(out=bias_bf[:, k, :], in_=bs[k].partition_broadcast(P))
+                    nc.sync.dma_start(out=bias_row[0:1, k, :], in_=bs[k].unsqueeze(0))
             elif what == "x":
                 xc, j0, n = x_tiles[c]
                 nc.sync.dma_start(out=xc[:], in_=xv[:, j0 : j0 + n, :])
@@ -159,14 +162,15 @@ def tile_loraqkvlinear_pa_t_kernel(
                 scales=w_planes[:, 2 * OUT : 3 * OUT],
                 in_=w_grouped[:, 2 * HID : 3 * HID],
             )
-            nc.gpsimd.tensor_scalar(
-                out=bias_f[:],
-                in0=bias_bf[:].unsqueeze(2).to_broadcast([P, KINDS, QUAD, OUT]),
-                scalar1=1.0,
-                scalar2=0.0,
-                op0=MULT,
-                op1=ADD,
-            )
+
+        def bias_pe():
+            pb = bank([P, KINDS, OUT], F32)
+            for k in range(KINDS):
+                nc.tensor.matmul(pb[:, k, :], lhsT=ones[:], rhs=bias_row[:, k, :], start=True, stop=True)
+            return pb
+
+        def bias_rest(pb):
+            nc.vector.tensor_copy(out=bias_f[:], in_=pb[:].unsqueeze(2).to_broadcast([P, KINDS, QUAD, OUT]))
 
         def x_src(j):
             xc, i = x_of[j]
@@ -254,6 +258,8 @@ def tile_loraqkvlinear_pa_t_kernel(
                 xats = txa_pe(g + 2)
             if g == -2:
                 wt = weights_pe()
+            if g == -1:
+                pb = bias_pe()
             if valid(g - 1):
                 base_out(g - 1, 1)
                 base_out(g - 1, 2)
@@ -268,6 +274,8 @@ def tile_loraqkvlinear_pa_t_kernel(
                 xaT[g + 2] = xa_t
             if g == -2:
                 weights_rest(wt)
+            if g == -1:
+                bias_rest(pb)
             if valid(g + 1):
                 ds = delta_pe(g + 1)
                 delta_out_vector(g + 1, 0, ds[0])

@@ -62,7 +62,7 @@ def tile_loraqkvlinear_pa_t_kernel(
         up_sb = consts.tile([P, KINDS, OUT], BF16, name="up_sb")
         bias_row = consts.tile([P, KINDS, OUT], BF16, name="bias_row")
         nc.vector.memset(bias_row[:], 0.0)
-        ones = consts.tile([P, P], BF16, name="ones")
+        ones = consts.tile([P, 4 * P], BF16, name="ones")
         nc.vector.memset(ones[:], 1.0)
 
         warm = consts.tile([P, 2], F32, name="warm")
@@ -144,7 +144,7 @@ def tile_loraqkvlinear_pa_t_kernel(
         w_grouped = consts.tile([P, KINDS * HID], BF16, name="w_grouped", align_bytes=64)
         w_codes = consts.tile([P, KINDS * OUT], U32, name="w_codes", align_bytes=64)
         w_planes = consts.tile([P, KINDS * OUT], U8, name="w_planes", align_bytes=64)
-        bias_f = consts.tile([P, KINDS, QUAD, OUT], F32, name="bias_f")
+        bias_f = consts.tile([P, 2, QUAD * OUT], F32, name="bias_f")
 
         def weights_pe():
             return [word_transposes([w_sb[:, 0, :], w_sb[:, 1, :]]), word_transposes([w_sb[:, 2, :]])]
@@ -166,11 +166,18 @@ def tile_loraqkvlinear_pa_t_kernel(
         def bias_pe():
             pb = bank([P, KINDS, OUT], F32)
             for k in range(KINDS):
-                nc.tensor.matmul(pb[:, k, :], lhsT=ones[:], rhs=bias_row[:, k, :], start=True, stop=True)
+                nc.tensor.matmul(pb[:, k, :], lhsT=ones[:, 0:P], rhs=bias_row[:, k, :], start=True, stop=True)
             return pb
 
         def bias_rest(pb):
-            nc.vector.tensor_copy(out=bias_f[:], in_=pb[:].unsqueeze(2).to_broadcast([P, KINDS, QUAD, OUT]))
+            nc.vector.tensor_copy(
+                out=bias_f[:, 0, :].rearrange("p (i c) -> p i c", i=2),
+                in_=pb[:, 0:2, :].rearrange("p k o -> p (k o)").unsqueeze(1).to_broadcast([P, 2, 2 * OUT]),
+            )
+            nc.vector.tensor_copy(
+                out=bias_f[:, 1, :].rearrange("p (i o) -> p i o", i=QUAD),
+                in_=pb[:, 2, :].unsqueeze(1).to_broadcast([P, QUAD, OUT]),
+            )
 
         def x_src(j):
             xc, i = x_of[j]
@@ -192,72 +199,118 @@ def tile_loraqkvlinear_pa_t_kernel(
 
         def delta_pe(g):
             out = []
-            for k in range(KINDS):
-                d = bank([P, QUAD, OUT], F32)
-                for i in range(QUAD):
-                    nc.tensor.matmul(
-                        d[:, i, :], lhsT=xaT[g][:, QUAD * k + i, :], rhs=up_sb[:, k, :], start=True, stop=True
-                    )
+            for h in range(2):
+                d = bank([P, 2, 2, OUT], F32)
+                for i in range(2):
+                    for k in range(2):
+                        nc.tensor.matmul(
+                            d[:, i, k, :],
+                            lhsT=xaT[g][:, QUAD * k + 2 * h + i, :],
+                            rhs=up_sb[:, k, :],
+                            start=True,
+                            stop=True,
+                        )
                 out.append(d)
+            d = bank([P, QUAD, OUT], F32)
+            for i in range(QUAD):
+                nc.tensor.matmul(d[:, i, :], lhsT=xaT[g][:, QUAD * 2 + i, :], rhs=up_sb[:, 2, :], start=True, stop=True)
+            out.append(d)
             return out
 
+        def mx_pass(out, g, i, lo, hi):
+            nc.tensor.matmul_mx(
+                out=out,
+                lhsT=codes[g][:, i * P : (i + 1) * P].bitcast(FP8X4),
+                lhsT_scale=planes[g][:, i * P : (i + 1) * P],
+                rhs=w_codes[:, lo:hi].bitcast(FP8X4),
+                rhs_scale=w_planes[:, lo:hi],
+                start=True,
+                stop=True,
+            )
+
         def base_pe(g):
-            for k in range(KINDS):
-                m = bank([P, QUAD, OUT], F32)
-                for i in range(QUAD):
-                    nc.tensor.matmul_mx(
-                        out=m[:, i, :],
-                        lhsT=codes[g][:, i * P : (i + 1) * P].bitcast(FP8X4),
-                        lhsT_scale=planes[g][:, i * P : (i + 1) * P],
-                        rhs=w_codes[:, k * OUT : (k + 1) * OUT].bitcast(FP8X4),
-                        rhs_scale=w_planes[:, k * OUT : (k + 1) * OUT],
-                        start=True,
-                        stop=True,
-                    )
-                mb[(g, k)] = m
+            for h in range(2):
+                m = bank([P, 2, 2 * OUT], F32)
+                for i in range(2):
+                    mx_pass(m[:, i, :], g, 2 * h + i, 0, 2 * OUT)
+                mb[(g, h)] = m
+            m = bank([P, QUAD, OUT], F32)
+            for i in range(QUAD):
+                mx_pass(m[:, i, :], g, i, 2 * OUT, 3 * OUT)
+            mb[(g, 2)] = m
+
+        def flat(ap):
+            if ap.ndim == 4:
+                return ap.rearrange("p a b c -> p (a b c)")
+            return ap.rearrange("p a b -> p (a b)")
 
         def delta_out_vector(g, k, d):
-            t = ring3.tile([P, QUAD, OUT], F32, name="t%d" % k)
+            t = ring3.tile([P, QUAD * OUT], F32, name="t%d" % k)
             nc.vector.scalar_tensor_tensor(
-                out=t[:].rearrange("p a b -> p (a b)"),
-                in0=d[:].rearrange("p a b -> p (a b)"),
-                scalar=SCALING,
-                in1=bias_f[:, k, :, :].rearrange("p a b -> p (a b)"),
-                op0=MULT,
-                op1=ADD,
+                out=t[:], in0=flat(d[:]), scalar=SCALING, in1=bias_f[:, k // 2, :], op0=MULT, op1=ADD
             )
             tt[(g, k)] = t
 
         def delta_out_scalar(g, k, d):
-            t = ring3.tile([P, QUAD, OUT], F32, name="t%d" % k)
-            nc.scalar.mul(out=t[:], in_=d[:], mul=SCALING)
+            t = ring3.tile([P, QUAD * OUT], F32, name="t%d" % k)
+            nc.scalar.mul(out=t[:], in_=flat(d[:]), mul=SCALING)
             tt[(g, k)] = t
 
         def bias_gpsimd(g, k):
             t = tt[(g, k)]
-            nc.gpsimd.tensor_tensor(out=t[:], in0=t[:], in1=bias_f[:, k, :, :], op=ADD)
+            nc.gpsimd.tensor_tensor(out=t[:], in0=t[:], in1=bias_f[:, k // 2, :], op=ADD)
+
+        def store(g, c, half, r, k):
+            if g >= NQ - TAPER:
+                j0 = g * QUAD
+                nc.sync.dma_start(out=ov[k][:, j0 : j0 + QUAD, :], in_=r[:, k, half * QUAD : (half + 1) * QUAD, :])
+            elif half == RES_TILES // QUAD - 1:
+                nc.sync.dma_start(out=ov[k][:, c * RES_TILES : (c + 1) * RES_TILES, :], in_=r[:, k, :, :])
 
         def base_out(g, k):
             c, half = divmod(g, RES_TILES // QUAD)
-            if (c, k) not in res:
-                res[(c, k)] = results.tile([P, RES_TILES, OUT], F32, name="res%d" % k)
-            r = res[(c, k)]
-            nc.vector.tensor_tensor(
-                out=r[:, half * QUAD : (half + 1) * QUAD, :], in0=mb[(g, k)][:], in1=tt[(g, k)][:], op=ADD
-            )
-            if g >= NQ - TAPER:
-                j0 = g * QUAD
-                nc.sync.dma_start(out=ov[k][:, j0 : j0 + QUAD, :], in_=r[:, half * QUAD : (half + 1) * QUAD, :])
-            elif half == RES_TILES // QUAD - 1:
-                nc.sync.dma_start(out=ov[k][:, c * RES_TILES : (c + 1) * RES_TILES, :], in_=r[:])
+            if c not in res:
+                res[c] = results.tile([P, KINDS, RES_TILES, OUT], F32, name="res")
+            r = res[c]
+            if k < 2:
+                j0 = half * QUAD + 2 * k
+                nc.vector.tensor_tensor(
+                    out=r[:, 0:2, j0 : j0 + 2, :].rearrange("p k i o -> p i k o"),
+                    in0=mb[(g, k)][:].rearrange("p i (k o) -> p i k o", k=2),
+                    in1=tt[(g, k)][:].rearrange("p (i k o) -> p i k o", i=2, k=2),
+                    op=ADD,
+                )
+                if k == 1:
+                    store(g, c, half, r, 0)
+                    store(g, c, half, r, 1)
+            else:
+                nc.vector.tensor_tensor(
+                    out=r[:, 2, half * QUAD : (half + 1) * QUAD, :],
+                    in0=mb[(g, k)][:],
+                    in1=tt[(g, k)][:].rearrange("p (i o) -> p i o", i=QUAD),
+                    op=ADD,
+                )
+                store(g, c, half, r, 2)
+
+        idle = bank([P, 4 * P], F32)
+
+        def warm(n):
+            for i in range(n):
+                nc.tensor.matmul(idle[:], lhsT=ones[:, 0:P], rhs=ones[:], start=True, stop=True)
+
+        warm(4)
 
         for g in range(-2, NQ + 1):
             if valid(g + 1):
                 xts = tx_pe(g + 1)
+            if g == -1:
+                warm(2)
             if valid(g + 2):
                 xats = txa_pe(g + 2)
             if g == -2:
+                warm(2)
                 wt = weights_pe()
+                warm(1)
             if g == -1:
                 pb = bias_pe()
             if valid(g - 1):

from contextlib import ExitStack

import concourse.mybir as mybir
from concourse.masks import make_identity

F32 = mybir.dt.float32
BF16 = mybir.dt.bfloat16
U32 = mybir.dt.uint32
U8 = mybir.dt.uint8
FP8X4 = mybir.dt.float8_e4m3fn_x4
ADD = mybir.AluOpType.add
MULT = mybir.AluOpType.mult

P = 128
TOKENS = 8192
HID = 512
OUT = 128
RANK = 128
KINDS = 3
NT = TOKENS // P
QUAD = 4
NQ = NT // QUAD
BANKS = 8
SCALING = 2.0

FLOPS = 2 * TOKENS * KINDS * OUT * (HID + RANK)

X_CHUNKS = [4, 4, 8, 8, 8, 8, 8, 8, 8]
XA_CHUNKS = [4, 4, 8, 16, 16, 16]
LOAD_ORDER = [
    ("xa", 0), ("w", 0), ("x", 0), ("up", 0), ("bias", 0), ("xa", 1), ("x", 1), ("xa", 2), ("x", 2), ("xa", 3), ("x", 3), ("x", 4), ("xa", 4), ("x", 5), ("x", 6), ("xa", 5), ("x", 7), ("x", 8),
]
RES_TILES = 8
TAPER = 2


def tile_loraqkvlinear_pa_t_kernel(
    tc, x, Wq, Wk, Wv, bq, bk, bv, xa_q, xa_k, xa_v, Bq, Bk, Bv, out_0, out_1, out_2
):
    nc = tc.nc
    xv = x.flatten_outer_dims().rearrange("(p j) h -> p j h", j=NT)
    xav = [a.flatten_outer_dims().rearrange("(p j) r -> p j r", j=NT) for a in (xa_q, xa_k, xa_v)]
    ov = [o.flatten_outer_dims().rearrange("(p j) o -> p j o", j=NT) for o in (out_0, out_1, out_2)]
    ws = (Wq, Wk, Wv)
    bs = (bq, bk, bv)
    ups = (Bq, Bk, Bv)

    with ExitStack() as ctx:
        consts = ctx.enter_context(tc.tile_pool(name="consts", bufs=1))
        inputs = ctx.enter_context(tc.tile_pool(name="inputs", bufs=1))
        ring2 = ctx.enter_context(tc.tile_pool(name="ring2", bufs=2))
        ring3 = ctx.enter_context(tc.tile_pool(name="ring3", bufs=3))
        results = ctx.enter_context(tc.tile_pool(name="results", bufs=5))
        psum = ctx.enter_context(tc.psum_pool(name="psum", bufs=1))
        ctx.enter_context(tc.manual_schedule())

        ident_f = consts.tile([P, P], F32, name="ident_f")
        make_identity(nc, ident_f[:])
        ident_b = consts.tile([P, P], BF16, name="ident_b")
        make_identity(nc, ident_b[:])

        up_sb = consts.tile([P, KINDS, OUT], BF16, name="up_sb")
        bias_row = consts.tile([P, KINDS, OUT], BF16, name="bias_row")
        nc.vector.memset(bias_row[:], 0.0)
        ones = consts.tile([P, 4 * P], BF16, name="ones")
        nc.vector.memset(ones[:], 1.0)

        warm = consts.tile([P, 2], F32, name="warm")
        nc.vector.memset(warm[:, 0:1], 0.0)
        nc.scalar.mul(out=warm[:, 1:2], in_=warm[:, 0:1], mul=SCALING)

        w_sb = inputs.tile([P, KINDS, HID], BF16, name="w_sb")
        x_of = {}
        xa_of = {}
        x_tiles = []
        j0 = 0
        for c, n in enumerate(X_CHUNKS):
            xc = inputs.tile([P, n, HID], BF16, name="x%d" % c)
            x_tiles.append((xc, j0, n))
            for i in range(n):
                x_of[j0 + i] = (xc, i)
            j0 += n
        xa_tiles = []
        j0 = 0
        for c, n in enumerate(XA_CHUNKS):
            group = []
            for k in range(KINDS):
                xac = inputs.tile([P, n, RANK], BF16, name="xa%d_%d" % (k, c))
                group.append(xac)
                for i in range(n):
                    xa_of[(k, j0 + i)] = (xac, i)
            xa_tiles.append((group, j0, n))
            j0 += n
        for what, c in LOAD_ORDER:
            if what == "w":
                for k in range(KINDS):
                    nc.sync.dma_start(out=w_sb[:, k, :], in_=ws[k])
            elif what == "up":
                for k in range(KINDS):
                    nc.sync.dma_start(out=up_sb[:, k, :], in_=ups[k])
            elif what == "bias":
                for k in range(KINDS):
                    nc.sync.dma_start(out=bias_row[0:1, k, :], in_=bs[k].unsqueeze(0))
            elif what == "x":
                xc, j0, n = x_tiles[c]
                nc.sync.dma_start(out=xc[:], in_=xv[:, j0 : j0 + n, :])
            else:
                group, j0, n = xa_tiles[c]
                for k in range(KINDS):
                    nc.sync.dma_start(out=group[k][:], in_=xav[k][:, j0 : j0 + n, :])

        count = [0]

        def bank(shape, dtype):
            i = count[0] % BANKS
            count[0] += 1
            return psum.tile(shape, dtype, name="bank%d" % i, tag="bank%d" % i)

        codes = {}
        planes = {}
        xaT = {}
        tt = {}
        mb = {}
        res = {}

        def valid(g):
            return 0 <= g < NQ

        def word_transposes(srcs):
            xt = bank([P, 2, 2, P], F32)
            for i, src in enumerate(srcs):
                words = src.bitcast(F32)
                for u in range(2):
                    nc.tensor.transpose(xt[:, i, u, :], words[:, u * P : (u + 1) * P], ident_f[:])
            return xt

        def copy_words(grouped, first, n, xt):
            view = grouped[:].bitcast(F32).rearrange("p (t r u) -> p t r u", r=P, u=2)
            nc.scalar.copy(
                out=view[:, first : first + n, :, :],
                in_=xt[:, 0:n, :, :].rearrange("p t u r -> p t r u"),
            )

        w_grouped = consts.tile([P, KINDS * HID], BF16, name="w_grouped", align_bytes=64)
        w_codes = consts.tile([P, KINDS * OUT], U32, name="w_codes", align_bytes=64)
        w_planes = consts.tile([P, KINDS * OUT], U8, name="w_planes", align_bytes=64)
        bias_f = consts.tile([P, 2, QUAD * OUT], F32, name="bias_f")

        def weights_pe():
            return [word_transposes([w_sb[:, 0, :], w_sb[:, 1, :]]), word_transposes([w_sb[:, 2, :]])]

        def weights_rest(wt):
            copy_words(w_grouped, 0, 2, wt[0])
            copy_words(w_grouped, 2, 1, wt[1])
            nc.vector.quantize_mx(
                out=w_codes[:, 0 : 2 * OUT].bitcast(FP8X4),
                scales=w_planes[:, 0 : 2 * OUT],
                in_=w_grouped[:, 0 : 2 * HID],
            )
            nc.vector.quantize_mx(
                out=w_codes[:, 2 * OUT : 3 * OUT].bitcast(FP8X4),
                scales=w_planes[:, 2 * OUT : 3 * OUT],
                in_=w_grouped[:, 2 * HID : 3 * HID],
            )

        def bias_pe():
            pb = bank([P, KINDS, OUT], F32)
            for k in range(KINDS):
                nc.tensor.matmul(pb[:, k, :], lhsT=ones[:, 0:P], rhs=bias_row[:, k, :], start=True, stop=True)
            return pb

        def bias_rest(pb):
            nc.vector.tensor_copy(
                out=bias_f[:, 0, :].rearrange("p (i c) -> p i c", i=2),
                in_=pb[:, 0:2, :].rearrange("p k o -> p (k o)").unsqueeze(1).to_broadcast([P, 2, 2 * OUT]),
            )
            nc.vector.tensor_copy(
                out=bias_f[:, 1, :].rearrange("p (i o) -> p i o", i=QUAD),
                in_=pb[:, 2, :].unsqueeze(1).to_broadcast([P, QUAD, OUT]),
            )

        def x_src(j):
            xc, i = x_of[j]
            return xc[:, i, :]

        def tx_pe(g):
            return [word_transposes([x_src(QUAD * g + 2 * h), x_src(QUAD * g + 2 * h + 1)]) for h in range(2)]

        def txa_pe(g):
            out = []
            for h in range(2):
                xat = bank([P, 6, P], BF16)
                for s in range(6):
                    k, i = divmod(6 * h + s, QUAD)
                    xac, loc = xa_of[(k, QUAD * g + i)]
                    nc.tensor.transpose(xat[:, s, :], xac[:, loc, :], ident_b[:])
                out.append(xat)
            return out

        def delta_pe(g):
            out = []
            for h in range(2):
                d = bank([P, 2, 2, OUT], F32)
                for i in range(2):
                    for k in range(2):
                        nc.tensor.matmul(
                            d[:, i, k, :],
                            lhsT=xaT[g][:, QUAD * k + 2 * h + i, :],
                            rhs=up_sb[:, k, :],
                            start=True,
                            stop=True,
                        )
                out.append(d)
            d = bank([P, QUAD, OUT], F32)
            for i in range(QUAD):
                nc.tensor.matmul(d[:, i, :], lhsT=xaT[g][:, QUAD * 2 + i, :], rhs=up_sb[:, 2, :], start=True, stop=True)
            out.append(d)
            return out

        def mx_pass(out, g, i, lo, hi):
            nc.tensor.matmul_mx(
                out=out,
                lhsT=codes[g][:, i * P : (i + 1) * P].bitcast(FP8X4),
                lhsT_scale=planes[g][:, i * P : (i + 1) * P],
                rhs=w_codes[:, lo:hi].bitcast(FP8X4),
                rhs_scale=w_planes[:, lo:hi],
                start=True,
                stop=True,
            )

        def base_pe(g):
            for h in range(2):
                m = bank([P, 2, 2 * OUT], F32)
                for i in range(2):
                    mx_pass(m[:, i, :], g, 2 * h + i, 0, 2 * OUT)
                mb[(g, h)] = m
            m = bank([P, QUAD, OUT], F32)
            for i in range(QUAD):
                mx_pass(m[:, i, :], g, i, 2 * OUT, 3 * OUT)
            mb[(g, 2)] = m

        def flat(ap):
            if ap.ndim == 4:
                return ap.rearrange("p a b c -> p (a b c)")
            return ap.rearrange("p a b -> p (a b)")

        def delta_out_vector(g, k, d):
            t = ring3.tile([P, QUAD * OUT], F32, name="t%d" % k)
            nc.vector.scalar_tensor_tensor(
                out=t[:], in0=flat(d[:]), scalar=SCALING, in1=bias_f[:, k // 2, :], op0=MULT, op1=ADD
            )
            tt[(g, k)] = t

        def delta_out_scalar(g, k, d):
            t = ring3.tile([P, QUAD * OUT], F32, name="t%d" % k)
            nc.scalar.mul(out=t[:], in_=flat(d[:]), mul=SCALING)
            tt[(g, k)] = t

        def bias_gpsimd(g, k):
            t = tt[(g, k)]
            nc.gpsimd.tensor_tensor(out=t[:], in0=t[:], in1=bias_f[:, k // 2, :], op=ADD)

        def store(g, c, half, r, k):
            if g >= NQ - TAPER:
                j0 = g * QUAD
                nc.sync.dma_start(out=ov[k][:, j0 : j0 + QUAD, :], in_=r[:, k, half * QUAD : (half + 1) * QUAD, :])
            elif half == RES_TILES // QUAD - 1:
                nc.sync.dma_start(out=ov[k][:, c * RES_TILES : (c + 1) * RES_TILES, :], in_=r[:, k, :, :])

        def base_out(g, k):
            c, half = divmod(g, RES_TILES // QUAD)
            if c not in res:
                res[c] = results.tile([P, KINDS, RES_TILES, OUT], F32, name="res")
            r = res[c]
            if k < 2:
                j0 = half * QUAD + 2 * k
                nc.vector.tensor_tensor(
                    out=r[:, 0:2, j0 : j0 + 2, :].rearrange("p k i o -> p i k o"),
                    in0=mb[(g, k)][:].rearrange("p i (k o) -> p i k o", k=2),
                    in1=tt[(g, k)][:].rearrange("p (i k o) -> p i k o", i=2, k=2),
                    op=ADD,
                )
                if k == 1:
                    store(g, c, half, r, 0)
                    store(g, c, half, r, 1)
            else:
                nc.vector.tensor_tensor(
                    out=r[:, 2, half * QUAD : (half + 1) * QUAD, :],
                    in0=mb[(g, k)][:],
                    in1=tt[(g, k)][:].rearrange("p (i o) -> p i o", i=QUAD),
                    op=ADD,
                )
                store(g, c, half, r, 2)

        idle = bank([P, 4 * P], F32)

        def warm(n):
            for i in range(n):
                nc.tensor.matmul(idle[:], lhsT=ones[:, 0:P], rhs=ones[:], start=True, stop=True)

        warm(4)

        for g in range(-2, NQ + 1):
            if valid(g + 1):
                xts = tx_pe(g + 1)
            if g == -1:
                warm(2)
            if valid(g + 2):
                xats = txa_pe(g + 2)
            if g == -2:
                warm(2)
                wt = weights_pe()
                warm(1)
            if g == -1:
                pb = bias_pe()
            if valid(g - 1):
                base_out(g - 1, 1)
                base_out(g - 1, 2)
            if valid(g + 1):
                grouped = ring2.tile([P, QUAD * HID], BF16, name="grouped", align_bytes=64)
                copy_words(grouped, 0, 2, xts[0])
                copy_words(grouped, 2, 2, xts[1])
            if valid(g + 2):
                xa_t = ring2.tile([P, KINDS * QUAD, P], BF16, name="xa_t")
                nc.scalar.copy(out=xa_t[:, 0:6, :].bitcast(F32), in_=xats[0][:].bitcast(F32))
                nc.scalar.copy(out=xa_t[:, 6:12, :].bitcast(F32), in_=xats[1][:].bitcast(F32))
                xaT[g + 2] = xa_t
            if g == -2:
                weights_rest(wt)
            if g == -1:
                bias_rest(pb)
            if valid(g + 1):
                ds = delta_pe(g + 1)
                delta_out_vector(g + 1, 0, ds[0])
                delta_out_scalar(g + 1, 1, ds[1])
                cw = ring2.tile([P, QUAD * P], U32, name="cw", align_bytes=64)
                pl = ring2.tile([P, QUAD * P], U8, name="pl", align_bytes=64)
                nc.vector.quantize_mx(out=cw[:].bitcast(FP8X4), scales=pl[:], in_=grouped[:])
                codes[g + 1] = cw
                planes[g + 1] = pl
                bias_gpsimd(g + 1, 1)
                delta_out_scalar(g + 1, 2, ds[2])
            if valid(g):
                base_pe(g)
            if valid(g + 1):
                bias_gpsimd(g + 1, 2)
            if valid(g):
                base_out(g, 0)
